import numpy as np
import ml_dtypes


def mxq(x, axis, fmt="e4m3"):
    dtype, down = {"e4m3": (ml_dtypes.float8_e4m3fn, 7), "e5m2": (ml_dtypes.float8_e5m2, 14)}[fmt]
    v = np.moveaxis(np.asarray(x, np.float32).astype(ml_dtypes.bfloat16).astype(np.float64), axis, -1)
    blocks = v.reshape(v.shape[:-1] + (-1, 32))
    amax = np.abs(blocks).max(-1, keepdims=True)
    byte = np.maximum(np.where(amax > 0, np.frexp(amax)[1] - 1 + 127, 0) - down, 1)
    scale = np.exp2(byte - 127.0)
    codes = (blocks / scale).astype(np.float32).astype(dtype).astype(np.float64)
    return np.moveaxis((codes * scale).reshape(v.shape), -1, axis)


WIDE = False


def mx_kscale(k):
    if not WIDE:
        return np.ones(k)
    levels = np.array([10, -10, 5, -5, 0])
    a = np.random.permutation(np.resize(levels, k // 512 * 4)).reshape(k // 512, 4)
    idx = np.arange(k)
    return np.exp2(a[idx // 512, idx % 128 // 32])


BF16 = ml_dtypes.bfloat16


def bf(x):
    return np.asarray(x, np.float32).astype(BF16)


def f64(x):
    return np.asarray(x).astype(np.float64)


B, S, D_MODEL, N_H, D_H, D_CQ, D_CKV, D_HR = 1, 512, 2048, 16, 128, 1024, 512, 128
ROPE_BASE = 10000.0


def rope_cos_sin(seq_len, dim):
    inv_freq = 1.0 / (ROPE_BASE ** (np.arange(0, dim, 2) / dim))
    ang = np.arange(seq_len)[:, None] * inv_freq[None, :]
    return np.cos(ang), np.sin(ang)


def rope(t, cos, sin):
    shp = t.shape
    d2 = shp[-1] // 2
    tr = t.reshape(shp[:-1] + (d2, 2))
    x0, x1 = tr[..., 0], tr[..., 1]
    bshape = (1, shp[1]) + (1,) * (x0.ndim - 3) + (d2,)
    cs, sn = cos.reshape(bshape), sin.reshape(bshape)
    return np.stack([x0 * cs - x1 * sn, x0 * sn + x1 * cs], axis=-1).reshape(shp)


def setup_inputs():
    s, t = mx_kscale(D_MODEL), mx_kscale(D_CQ)
    return {"h": bf(np.random.standard_normal((B, S, D_MODEL)) * s),
            "w_cq": bf(np.random.standard_normal((D_MODEL, D_CQ)) / np.sqrt(D_MODEL) / s[:, None] * t),
            "w_q": bf(np.random.standard_normal((D_CQ, N_H * D_H)) / np.sqrt(D_CQ) / t[:, None]),
            "w_qr": bf(np.random.standard_normal((D_CQ, N_H * D_HR)) / np.sqrt(D_CQ) / t[:, None])}


def reference(h, w_cq, w_q, w_qr):
    cos, sin = rope_cos_sin(S, D_HR)
    c_q = mxq(f64(h), 2, "e4m3") @ mxq(f64(w_cq), 0, "e4m3")
    cq = mxq(c_q, 2, "e4m3")
    q_c = (cq @ mxq(f64(w_q), 0, "e4m3")).reshape(B, S, N_H, D_H).transpose(0, 2, 1, 3)
    q_r = rope((cq @ mxq(f64(w_qr), 0, "e4m3")).reshape(B, S, N_H, D_HR), cos, sin).transpose(0, 2, 1, 3)
    return np.concatenate([q_c, q_r], axis=-1)

@@ -1,0 +1,332 @@
+import math
+from contextlib import ExitStack
+
+import concourse.mybir as mybir
+from concourse.masks import make_identity
+
+F32 = mybir.dt.float32
+BF16 = mybir.dt.bfloat16
+I32 = mybir.dt.int32
+U32 = mybir.dt.uint32
+U8 = mybir.dt.uint8
+FP8X4 = mybir.dt.float8_e4m3fn_x4
+ALU = mybir.AluOpType
+ACT = mybir.ActivationFunctionType
+
+P = 128
+PACK = 4
+K_PASS = P * PACK
+
+S = 512
+D_MODEL = 2048
+D_CQ = 1024
+HEADS = 16
+D_HEAD = 128
+PAIRS = D_HEAD // 2
+ROPE_BASE = 10000.0
+
+S_TILES = S // P
+PASSES_1 = D_MODEL // K_PASS
+PASSES_2 = D_CQ // K_PASS
+PIECE = 512
+LOAD_COLS = 2 * PIECE
+GROUP_HEADS = PIECE // D_HEAD
+GROUPS = HEADS // GROUP_HEADS
+
+RAW_BUFS = 8
+VECTOR_COLS_W_CQ = 256
+VECTOR_COLS_BY_HALF = (192, 32)
+
+TWO_PI = 2.0 * math.pi
+TWO_PI_HI = 6.28125
+TWO_PI_MID = round((TWO_PI - TWO_PI_HI) * 2.0**20) / 2.0**20
+TWO_PI_LO = TWO_PI - TWO_PI_HI - TWO_PI_MID
+ROUND_MAGIC = 1.5 * 2.0**23
+
+FLOPS = 2 * S * D_MODEL * D_CQ + 2 * S * D_CQ * 2 * HEADS * D_HEAD
+
+
+def build_rope_tables(nc, pool):
+    shape = [P, S_TILES, PAIRS]
+    position_int = pool.tile([P, S_TILES], I32)
+    nc.gpsimd.iota(position_int[:], pattern=[[1, S_TILES]], base=0, channel_multiplier=S_TILES)
+    position = pool.tile([P, S_TILES], F32)
+    nc.vector.tensor_copy(out=position[:], in_=position_int[:])
+
+    frequency = pool.tile([P, PAIRS], F32)
+    nc.vector.memset(frequency[:, 0:1], 1.0)
+    filled = 1
+    while filled < PAIRS:
+        nc.vector.tensor_scalar_mul(
+            out=frequency[:, filled : 2 * filled],
+            in0=frequency[:, 0:filled],
+            scalar1=ROPE_BASE ** (-2.0 * filled / D_HEAD),
+        )
+        filled *= 2
+    angle = pool.tile(shape, F32)
+    nc.vector.tensor_tensor(
+        out=angle[:],
+        in0=frequency[:].unsqueeze(1).to_broadcast(shape),
+        in1=position[:].unsqueeze(2).to_broadcast(shape),
+        op=ALU.mult,
+    )
+
+    turns = pool.tile(shape, F32)
+    nc.vector.tensor_scalar(
+        out=turns[:], in0=angle[:], scalar1=1.0 / TWO_PI, scalar2=ROUND_MAGIC, op0=ALU.mult, op1=ALU.add
+    )
+    nc.vector.tensor_scalar(
+        out=turns[:], in0=turns[:], scalar1=ROUND_MAGIC, scalar2=None, op0=ALU.subtract
+    )
+    for part in (TWO_PI_HI, TWO_PI_MID, TWO_PI_LO):
+        nc.vector.scalar_tensor_tensor(
+            out=angle[:], in0=turns[:], scalar=-part, in1=angle[:], op0=ALU.mult, op1=ALU.add
+        )
+
+    sin_half = pool.tile(shape, F32)
+    nc.scalar.activation(out=sin_half[:], in_=angle[:], func=ACT.Sin, scale=0.5)
+    sin_quarter = pool.tile(shape, F32)
+    nc.scalar.activation(out=sin_quarter[:], in_=angle[:], func=ACT.Sin, scale=0.25)
+
+    square_half = pool.tile(shape, F32)
+    nc.vector.tensor_tensor(out=square_half[:], in0=sin_half[:], in1=sin_half[:], op=ALU.mult)
+    cos_twice = pool.tile([P, S_TILES, D_HEAD], F32)
+    nc.vector.tensor_scalar(
+        out=cos_twice[:].rearrange("p a (i e) -> p (a i) e", e=2),
+        in0=square_half[:].rearrange("p a i -> p (a i)").unsqueeze(2).to_broadcast([P, S_TILES * PAIRS, 2]),
+        scalar1=-2.0,
+        scalar2=1.0,
+        op0=ALU.mult,
+        op1=ALU.add,
+    )
+    cos_half = pool.tile(shape, F32)
+    nc.vector.tensor_tensor(out=cos_half[:], in0=sin_quarter[:], in1=sin_quarter[:], op=ALU.mult)
+    nc.vector.tensor_scalar(
+        out=cos_half[:], in0=cos_half[:], scalar1=-2.0, scalar2=1.0, op0=ALU.mult, op1=ALU.add
+    )
+    sin_plus = pool.tile(shape, F32)
+    nc.vector.scalar_tensor_tensor(
+        out=sin_plus[:], in0=sin_half[:], scalar=2.0, in1=cos_half[:], op0=ALU.mult, op1=ALU.mult
+    )
+    sin_minus = pool.tile(shape, F32)
+    nc.vector.scalar_tensor_tensor(
+        out=sin_minus[:], in0=sin_half[:], scalar=-2.0, in1=cos_half[:], op0=ALU.mult, op1=ALU.mult
+    )
+    return cos_twice, sin_plus, sin_minus
+
+
+def quantise(nc, codes, scales, grouped):
+    nc.vector.quantize_mx(out=codes.bitcast(FP8X4), scales=scales, in_=grouped)
+
+
+def quantise_weight_piece(nc, stage, keep, raw_piece, vector_cols, label):
+    grouped = stage.tile([P, PIECE, PACK], BF16, align_bytes=64)
+    nc.vector.tensor_copy(
+        out=grouped[:, :vector_cols, :].rearrange("p (w i) t -> p w t i", i=4),
+        in_=raw_piece[:, :, :vector_cols].rearrange("p t (w i) -> p w t i", i=4),
+    )
+    nc.scalar.copy(
+        out=grouped[:, vector_cols:, :].rearrange("p (w i) t -> p w t i", i=4),
+        in_=raw_piece[:, :, vector_cols:].rearrange("p t (w i) -> p w t i", i=4),
+    )
+    codes = keep.tile([P, PIECE], U32, align_bytes=64, name=label + "_codes")
+    scales = keep.tile([P, PIECE], U8, align_bytes=64, name=label + "_scales")
+    quantise(nc, codes[:], scales[:], grouped[:].rearrange("p w t -> p (w t)"))
+    return codes, scales
+
+
+def multiply_mx(nc, acc, stationary, moving, first, last):
+    nc.tensor.matmul_mx(
+        out=acc,
+        lhsT=stationary[0].bitcast(FP8X4),
+        lhsT_scale=stationary[1],
+        rhs=moving[0].bitcast(FP8X4),
+        rhs_scale=moving[1],
+        start=first,
+        stop=last,
+    )
+
+
+def columns(operand, start, width):
+    return operand[0][:, start : start + width], operand[1][:, start : start + width]
+
+
+def tile_mla_pa_kernel(tc, h, w_cq, w_q, w_qr, out):
+    nc = tc.nc
+    with ExitStack() as ctx:
+        const = ctx.enter_context(tc.tile_pool(name="const", bufs=1))
+        keep = ctx.enter_context(tc.tile_pool(name="keep", bufs=1))
+        raw_pool = ctx.enter_context(tc.tile_pool(name="raw_pool", bufs=RAW_BUFS))
+        stage = ctx.enter_context(tc.tile_pool(name="stage", bufs=4))
+        small_stage = ctx.enter_context(tc.tile_pool(name="small_stage", bufs=2))
+        psum = ctx.enter_context(tc.psum_pool(name="psum", bufs=8))
+
+        identity = const.tile([P, P], F32)
+        make_identity(nc, identity[:])
+        cos_twice, sin_plus, sin_minus = build_rope_tables(nc, const)
+
+        h_rows = h.flatten_outer_dims().rearrange("(p a) k -> p a k", a=S_TILES)
+        h_mx = []
+        with tc.tile_pool(name="h_pool", bufs=S_TILES) as h_pool, tc.tile_pool(name="h_stage", bufs=2) as h_stage:
+            h_raw = []
+            for a in range(S_TILES):
+                h_tile = h_pool.tile([P, D_MODEL], BF16)
+                nc.sync.dma_start(out=h_tile[:], in_=h_rows[:, a, :])
+                h_raw.append(h_tile)
+            for a in range(S_TILES):
+                h_words = h_raw[a][:].bitcast(F32)
+                h_grouped = h_stage.tile([P, PASSES_1, P, PACK], BF16, align_bytes=64)
+                for b in range(PASSES_1 // 2):
+                    flipped = psum.tile([P, 4, P], F32, tag="bank")
+                    for j in range(4):
+                        first_word = (4 * b + j) * P
+                        nc.tensor.transpose(flipped[:, j, :], h_words[:, first_word : first_word + P], identity[:])
+                    nc.scalar.copy(
+                        out=h_grouped[:, 2 * b : 2 * b + 2].bitcast(F32),
+                        in_=flipped[:].rearrange("q (c u) s -> q c s u", u=2),
+                    )
+                codes = keep.tile([P, PASSES_1 * P], U32, align_bytes=64, name="h_codes%d" % a)
+                scales = keep.tile([P, PASSES_1 * P], U8, align_bytes=64, name="h_scales%d" % a)
+                quantise(nc, codes[:], scales[:], h_grouped[:].rearrange("q c s t -> q (c s t)"))
+                h_mx.append((codes, scales))
+        rope_pool = ctx.enter_context(tc.tile_pool(name="rope_pool", bufs=4, reuse_waits="tile"))
+        result_pool = ctx.enter_context(tc.tile_pool(name="result_pool", bufs=3, reuse_waits="tile"))
+
+        w_cq_rows = w_cq.rearrange("(c u p e) n -> c p u e n", c=PASSES_1, u=2, e=2)
+        sources = [w_cq_rows[c] for c in range(PASSES_1)]
+        for half in range(HEADS * D_HEAD // LOAD_COLS):
+            for weight in (w_q, w_qr):
+                rows = weight.rearrange("(g t p) n -> g p t n", g=PASSES_2, t=PACK)
+                for g in range(PASSES_2):
+                    sources.append(rows[g][:, :, half * LOAD_COLS : (half + 1) * LOAD_COLS])
+        raw_tiles = []
+
+        def load_next_weights():
+            if len(raw_tiles) < len(sources):
+                source = sources[len(raw_tiles)]
+                raw = raw_pool.tile([P, PACK, LOAD_COLS], BF16)
+                if source.ndim == 4:
+                    nc.sync.dma_start(out=raw[:].rearrange("p (u e) n -> p u e n", e=2), in_=source)
+                else:
+                    nc.sync.dma_start(out=raw[:], in_=source)
+                raw_tiles.append(raw)
+
+        for j in range(RAW_BUFS):
+            load_next_weights()
+
+        w_cq_mx = []
+        for c in range(PASSES_1):
+            raw = raw_tiles[c]
+            w_cq_mx.append(
+                [
+                    quantise_weight_piece(
+                        nc, stage, keep, raw[:, :, g * PIECE : (g + 1) * PIECE], VECTOR_COLS_W_CQ, "w_cq%d%d" % (c, g)
+                    )
+                    for g in range(PASSES_2)
+                ]
+            )
+            load_next_weights()
+
+        c_q_mx = []
+        for a in range(S_TILES):
+            c_q_grouped = small_stage.tile([P, PASSES_2, P, PACK], BF16, align_bytes=64)
+            for g in range(PASSES_2):
+                c_q_bank = psum.tile([P, PACK, P], F32, tag="bank")
+                for t in range(PACK):
+                    for c in range(PASSES_1):
+                        multiply_mx(
+                            nc,
+                            c_q_bank[:, t, :],
+                            columns(w_cq_mx[c][g], t * P, P),
+                            columns(h_mx[a], c * P, P),
+                            first=(c == 0),
+                            last=(c == PASSES_1 - 1),
+                        )
+                nc.scalar.copy(out=c_q_grouped[:, g], in_=c_q_bank[:].rearrange("m t s -> m s t"))
+            codes = keep.tile([P, PASSES_2 * P], U32, align_bytes=64, name="c_q_codes%d" % a)
+            scales = keep.tile([P, PASSES_2 * P], U8, align_bytes=64, name="c_q_scales%d" % a)
+            quantise(nc, codes[:], scales[:], c_q_grouped[:].rearrange("m g s t -> m (g s t)"))
+            c_q_mx.append((codes, scales))
+
+        def quantise_group_weights(group):
+            half, part = divmod(group, LOAD_COLS // PIECE)
+            first_raw = PASSES_1 + half * 2 * PASSES_2
+            pieces = []
+            for j in range(2 * PASSES_2):
+                raw = raw_tiles[first_raw + j]
+                pieces.append(
+                    quantise_weight_piece(
+                        nc,
+                        stage,
+                        keep,
+                        raw[:, :, part * PIECE : (part + 1) * PIECE],
+                        VECTOR_COLS_BY_HALF[half],
+                        "w%d%d" % (group, j),
+                    )
+                )
+            return pieces[:PASSES_2], pieces[PASSES_2:]
+
+        def multiply_by_weights(a, weights):
+            bank = psum.tile([P, GROUP_HEADS, D_HEAD], F32, tag="bank")
+            for g in range(PASSES_2):
+                multiply_mx(
+                    nc,
+                    bank[:].rearrange("p n d -> p (n d)"),
+                    columns(c_q_mx[a], g * P, P),
+                    columns(weights[g], 0, PIECE),
+                    first=(g == 0),
+                    last=(g == PASSES_2 - 1),
+                )
+            return bank
+
+        def rope_products(a, u_bank):
+            pairs = [P, GROUP_HEADS, PAIRS]
+            u_pairs = u_bank[:].rearrange("p n (i e) -> p n i e", e=2)
+            by_cos = rope_pool.tile([P, GROUP_HEADS, D_HEAD], F32)
+            nc.vector.tensor_tensor(
+                out=by_cos[:],
+                in0=u_bank[:],
+                in1=cos_twice[:, a, :].unsqueeze(1).to_broadcast([P, GROUP_HEADS, D_HEAD]),
+                op=ALU.mult,
+            )
+            by_sin = rope_pool.tile([P, GROUP_HEADS, 2, PAIRS], F32)
+            nc.vector.tensor_tensor(
+                out=by_sin[:, :, 0, :],
+                in0=u_pairs[:, :, :, 1],
+                in1=sin_minus[:, a, :].unsqueeze(1).to_broadcast(pairs),
+                op=ALU.mult,
+            )
+            nc.vector.tensor_tensor(
+                out=by_sin[:, :, 1, :],
+                in0=u_pairs[:, :, :, 0],
+                in1=sin_plus[:, a, :].unsqueeze(1).to_broadcast(pairs),
+                op=ALU.mult,
+            )
+            return by_cos, by_sin
+
+        out_rows = out.rearrange("b n (p a) d -> p (b n) a d", a=S_TILES)
+        group_weights = [quantise_group_weights(0)]
+        for group in range(GROUPS):
+            if group + 1 < GROUPS:
+                group_weights.append(quantise_group_weights(group + 1))
+            w_q_mx, w_qr_mx = group_weights[group]
+            for first_a in range(0, S_TILES, 2):
+                result = result_pool.tile([P, GROUP_HEADS, 2, 2 * D_HEAD], F32)
+                products = []
+                for x in range(2):
+                    a_bank = multiply_by_weights(first_a + x, w_q_mx)
+                    u_bank = multiply_by_weights(first_a + x, w_qr_mx)
+                    nc.scalar.copy(out=result[:, :, x, 0:D_HEAD], in_=a_bank[:])
+                    products.append(rope_products(first_a + x, u_bank))
+                for x in range(2):
+                    by_cos, by_sin = products[x]
+                    nc.vector.tensor_tensor(
+                        out=result[:, :, x, D_HEAD:].rearrange("p n (i e) -> p n i e", e=2),
+                        in0=by_cos[:].rearrange("p n (i e) -> p n i e", e=2),
+                        in1=by_sin[:].rearrange("p n e i -> p n i e"),
+                        op=ALU.add,
+                    )
+                nc.sync.dma_start(
+                    out=out_rows[:, group * GROUP_HEADS : (group + 1) * GROUP_HEADS, first_a : first_a + 2, :],
+                    in_=result[:],
+                )

@@ -30,23 +30,26 @@ PASSES_1 = D_MODEL // K_PASS
 PASSES_2 = D_CQ // K_PASS
 PIECE = 512
 LOAD_COLS = 2 * PIECE
+PARTS = LOAD_COLS // PIECE
 GROUP_HEADS = PIECE // D_HEAD
-GROUPS = HEADS // GROUP_HEADS
+HALVES = HEADS * D_HEAD // LOAD_COLS
+
+C_Q_BANKS = S_TILES * PASSES_2
+PIECES = 2 * PASSES_2 * HALVES * PARTS
+STEPS = S_TILES * HALVES * PARTS
+U_LAG = 4
+A_LAG = 8
 
 RAW_BUFS = 8
-VECTOR_COLS_W_CQ = 256
-VECTOR_COLS_BY_HALF = (192, 32)
+VECTOR_COLS_BEFORE_ROPE = 256
+VECTOR_COLS_BESIDE_ROPE = 48
 
-TWO_PI = 2.0 * math.pi
-TWO_PI_HI = 6.28125
-TWO_PI_MID = round((TWO_PI - TWO_PI_HI) * 2.0**20) / 2.0**20
-TWO_PI_LO = TWO_PI - TWO_PI_HI - TWO_PI_MID
 ROUND_MAGIC = 1.5 * 2.0**23
 
 FLOPS = 2 * S * D_MODEL * D_CQ + 2 * S * D_CQ * 2 * HEADS * D_HEAD
 
 
-def build_rope_tables(nc, pool):
+def rope_half_angles(nc, pool):
     shape = [P, S_TILES, PAIRS]
     position_int = pool.tile([P, S_TILES], I32)
     nc.gpsimd.iota(position_int[:], pattern=[[1, S_TILES]], base=0, channel_multiplier=S_TILES)
@@ -63,76 +66,53 @@ def build_rope_tables(nc, pool):
             scalar1=ROPE_BASE ** (-2.0 * filled / D_HEAD),
         )
         filled *= 2
-    angle = pool.tile(shape, F32)
-    nc.vector.tensor_tensor(
-        out=angle[:],
-        in0=frequency[:].unsqueeze(1).to_broadcast(shape),
-        in1=position[:].unsqueeze(2).to_broadcast(shape),
-        op=ALU.mult,
-    )
-
     turns = pool.tile(shape, F32)
-    nc.vector.tensor_scalar(
-        out=turns[:], in0=angle[:], scalar1=1.0 / TWO_PI, scalar2=ROUND_MAGIC, op0=ALU.mult, op1=ALU.add
+    nc.vector.scalar_tensor_tensor(
+        out=turns[:],
+        in0=frequency[:].unsqueeze(1).to_broadcast(shape),
+        scalar=1.0 / (2.0 * math.pi),
+        in1=position[:].unsqueeze(2).to_broadcast(shape),
+        op0=ALU.mult,
+        op1=ALU.mult,
     )
+    whole_turns = pool.tile(shape, F32)
     nc.vector.tensor_scalar(
-        out=turns[:], in0=turns[:], scalar1=ROUND_MAGIC, scalar2=None, op0=ALU.subtract
+        out=whole_turns[:], in0=turns[:], scalar1=ROUND_MAGIC, scalar2=ROUND_MAGIC, op0=ALU.add, op1=ALU.subtract
     )
-    for part in (TWO_PI_HI, TWO_PI_MID, TWO_PI_LO):
-        nc.vector.scalar_tensor_tensor(
-            out=angle[:], in0=turns[:], scalar=-part, in1=angle[:], op0=ALU.mult, op1=ALU.add
-        )
+    nc.vector.tensor_tensor(out=turns[:], in0=turns[:], in1=whole_turns[:], op=ALU.subtract)
 
     sin_half = pool.tile(shape, F32)
-    nc.scalar.activation(out=sin_half[:], in_=angle[:], func=ACT.Sin, scale=0.5)
+    nc.scalar.activation(out=sin_half[:], in_=turns[:], func=ACT.Sin, scale=math.pi)
     sin_quarter = pool.tile(shape, F32)
-    nc.scalar.activation(out=sin_quarter[:], in_=angle[:], func=ACT.Sin, scale=0.25)
-
-    square_half = pool.tile(shape, F32)
-    nc.vector.tensor_tensor(out=square_half[:], in0=sin_half[:], in1=sin_half[:], op=ALU.mult)
+    nc.scalar.activation(out=sin_quarter[:], in_=turns[:], func=ACT.Sin, scale=math.pi / 2.0)
+    square = pool.tile(shape, F32)
+    nc.scalar.activation(out=square[:], in_=sin_half[:], func=ACT.Square)
     cos_twice = pool.tile([P, S_TILES, D_HEAD], F32)
-    nc.vector.tensor_scalar(
+    nc.scalar.activation(
         out=cos_twice[:].rearrange("p a (i e) -> p (a i) e", e=2),
-        in0=square_half[:].rearrange("p a i -> p (a i)").unsqueeze(2).to_broadcast([P, S_TILES * PAIRS, 2]),
-        scalar1=-2.0,
-        scalar2=1.0,
-        op0=ALU.mult,
-        op1=ALU.add,
+        in_=square[:].rearrange("p a i -> p (a i)").unsqueeze(2).to_broadcast([P, S_TILES * PAIRS, 2]),
+        func=ACT.Copy,
+        scale=-2.0,
+        bias=1.0,
     )
     cos_half = pool.tile(shape, F32)
-    nc.vector.tensor_tensor(out=cos_half[:], in0=sin_quarter[:], in1=sin_quarter[:], op=ALU.mult)
-    nc.vector.tensor_scalar(
-        out=cos_half[:], in0=cos_half[:], scalar1=-2.0, scalar2=1.0, op0=ALU.mult, op1=ALU.add
-    )
-    sin_plus = pool.tile(shape, F32)
-    nc.vector.scalar_tensor_tensor(
-        out=sin_plus[:], in0=sin_half[:], scalar=2.0, in1=cos_half[:], op0=ALU.mult, op1=ALU.mult
-    )
-    sin_minus = pool.tile(shape, F32)
-    nc.vector.scalar_tensor_tensor(
-        out=sin_minus[:], in0=sin_half[:], scalar=-2.0, in1=cos_half[:], op0=ALU.mult, op1=ALU.mult
-    )
-    return cos_twice, sin_plus, sin_minus
+    nc.scalar.activation(out=cos_half[:], in_=sin_quarter[:], func=ACT.Square)
+    nc.scalar.activation(out=cos_half[:], in_=cos_half[:], func=ACT.Copy, scale=-2.0, bias=1.0)
+    return sin_half, cos_half, cos_twice
 
 
-def quantise(nc, codes, scales, grouped):
-    nc.vector.quantize_mx(out=codes.bitcast(FP8X4), scales=scales, in_=grouped)
+def quantise(nc, operand, grouped):
+    nc.vector.quantize_mx(out=operand[0][:].bitcast(FP8X4), scales=operand[1][:], in_=grouped)
 
 
-def quantise_weight_piece(nc, stage, keep, raw_piece, vector_cols, label):
-    grouped = stage.tile([P, PIECE, PACK], BF16, align_bytes=64)
-    nc.vector.tensor_copy(
-        out=grouped[:, :vector_cols, :].rearrange("p (w i) t -> p w t i", i=4),
-        in_=raw_piece[:, :, :vector_cols].rearrange("p t (w i) -> p w t i", i=4),
-    )
-    nc.scalar.copy(
-        out=grouped[:, vector_cols:, :].rearrange("p (w i) t -> p w t i", i=4),
-        in_=raw_piece[:, :, vector_cols:].rearrange("p t (w i) -> p w t i", i=4),
-    )
-    codes = keep.tile([P, PIECE], U32, align_bytes=64, name=label + "_codes")
-    scales = keep.tile([P, PIECE], U8, align_bytes=64, name=label + "_scales")
-    quantise(nc, codes[:], scales[:], grouped[:].rearrange("p w t -> p (w t)"))
+def mx_operand(pool, width, label):
+    codes = pool.tile([P, width], U32, align_bytes=64, name=label + "_codes")
+    scales = pool.tile([P, width], U8, align_bytes=64, name=label + "_scales")
     return codes, scales
+
+
+def columns(operand, start, width):
+    return operand[0][:, start : start + width], operand[1][:, start : start + width]
 
 
 def multiply_mx(nc, acc, stationary, moving, first, last):
@@ -147,23 +127,33 @@ def multiply_mx(nc, acc, stationary, moving, first, last):
     )
 
 
-def columns(operand, start, width):
-    return operand[0][:, start : start + width], operand[1][:, start : start + width]
+def regroup(nc, grouped, raw_piece, vector_cols):
+    nc.vector.tensor_copy(
+        out=grouped[:, :vector_cols, :].rearrange("p (w i) t -> p w t i", i=4),
+        in_=raw_piece[:, :, :vector_cols].rearrange("p t (w i) -> p w t i", i=4),
+    )
+    nc.scalar.copy(
+        out=grouped[:, vector_cols:, :].rearrange("p (w i) t -> p w t i", i=4),
+        in_=raw_piece[:, :, vector_cols:].rearrange("p t (w i) -> p w t i", i=4),
+    )
 
 
 def tile_mla_pa_kernel(tc, h, w_cq, w_q, w_qr, out):
     nc = tc.nc
     with ExitStack() as ctx:
+        ctx.enter_context(tc.manual_schedule())
         const = ctx.enter_context(tc.tile_pool(name="const", bufs=1))
         keep = ctx.enter_context(tc.tile_pool(name="keep", bufs=1))
         raw_pool = ctx.enter_context(tc.tile_pool(name="raw_pool", bufs=RAW_BUFS))
         stage = ctx.enter_context(tc.tile_pool(name="stage", bufs=4))
-        small_stage = ctx.enter_context(tc.tile_pool(name="small_stage", bufs=2))
-        psum = ctx.enter_context(tc.psum_pool(name="psum", bufs=8))
+        c_q_stage = ctx.enter_context(tc.tile_pool(name="c_q_stage", bufs=2))
+        psum_u = ctx.enter_context(tc.psum_pool(name="psum_u", bufs=4))
+        psum_a = ctx.enter_context(tc.psum_pool(name="psum_a", bufs=2))
+        psum_c_q = ctx.enter_context(tc.psum_pool(name="psum_c_q", bufs=2))
 
         identity = const.tile([P, P], F32)
         make_identity(nc, identity[:])
-        cos_twice, sin_plus, sin_minus = build_rope_tables(nc, const)
+        sin_half, cos_half, cos_twice = rope_half_angles(nc, const)
 
         h_rows = h.flatten_outer_dims().rearrange("(p a) k -> p a k", a=S_TILES)
         h_mx = []
@@ -173,11 +163,34 @@ def tile_mla_pa_kernel(tc, h, w_cq, w_q, w_qr, out):
                 h_tile = h_pool.tile([P, D_MODEL], BF16)
                 nc.sync.dma_start(out=h_tile[:], in_=h_rows[:, a, :])
                 h_raw.append(h_tile)
+
+            w_cq_rows = w_cq.rearrange("(c u p e) n -> c p u e n", c=PASSES_1, u=2, e=2)
+            sources = [w_cq_rows[c] for c in range(PASSES_1)]
+            for half in range(HALVES):
+                for weight in (w_qr, w_q):
+                    rows = weight.rearrange("(g t p) n -> g p t n", g=PASSES_2, t=PACK)
+                    for g in range(PASSES_2):
+                        sources.append(rows[g][:, :, half * LOAD_COLS : (half + 1) * LOAD_COLS])
+            raw_tiles = []
+
+            def load_next_weights():
+                if len(raw_tiles) < len(sources):
+                    source = sources[len(raw_tiles)]
+                    raw = raw_pool.tile([P, PACK, LOAD_COLS], BF16)
+                    if source.ndim == 4:
+                        nc.sync.dma_start(out=raw[:].rearrange("p (u e) n -> p u e n", e=2), in_=source)
+                    else:
+                        nc.sync.dma_start(out=raw[:], in_=source)
+                    raw_tiles.append(raw)
+
+            for j in range(RAW_BUFS):
+                load_next_weights()
+
             for a in range(S_TILES):
                 h_words = h_raw[a][:].bitcast(F32)
                 h_grouped = h_stage.tile([P, PASSES_1, P, PACK], BF16, align_bytes=64)
                 for b in range(PASSES_1 // 2):
-                    flipped = psum.tile([P, 4, P], F32, tag="bank")
+                    flipped = psum_u.tile([P, 4, P], F32, tag="u_bank")
                     for j in range(4):
                         first_word = (4 * b + j) * P
                         nc.tensor.transpose(flipped[:, j, :], h_words[:, first_word : first_word + P], identity[:])
@@ -185,101 +198,96 @@ def tile_mla_pa_kernel(tc, h, w_cq, w_q, w_qr, out):
                         out=h_grouped[:, 2 * b : 2 * b + 2].bitcast(F32),
                         in_=flipped[:].rearrange("q (c u) s -> q c s u", u=2),
                     )
-                codes = keep.tile([P, PASSES_1 * P], U32, align_bytes=64, name="h_codes%d" % a)
-                scales = keep.tile([P, PASSES_1 * P], U8, align_bytes=64, name="h_scales%d" % a)
-                quantise(nc, codes[:], scales[:], h_grouped[:].rearrange("q c s t -> q (c s t)"))
-                h_mx.append((codes, scales))
-        rope_pool = ctx.enter_context(tc.tile_pool(name="rope_pool", bufs=4, reuse_waits="tile"))
-        result_pool = ctx.enter_context(tc.tile_pool(name="result_pool", bufs=3, reuse_waits="tile"))
+                h_mx.append(mx_operand(keep, PASSES_1 * P, "h%d" % a))
+                quantise(nc, h_mx[a], h_grouped[:].rearrange("q c s t -> q (c s t)"))
+        rope_pool = ctx.enter_context(tc.tile_pool(name="rope_pool", bufs=3, reuse_waits="tile"))
+        result_pool = ctx.enter_context(tc.tile_pool(name="result_pool", bufs=5, reuse_waits="tile"))
 
-        w_cq_rows = w_cq.rearrange("(c u p e) n -> c p u e n", c=PASSES_1, u=2, e=2)
-        sources = [w_cq_rows[c] for c in range(PASSES_1)]
-        for half in range(HEADS * D_HEAD // LOAD_COLS):
-            for weight in (w_q, w_qr):
-                rows = weight.rearrange("(g t p) n -> g p t n", g=PASSES_2, t=PACK)
-                for g in range(PASSES_2):
-                    sources.append(rows[g][:, :, half * LOAD_COLS : (half + 1) * LOAD_COLS])
-        raw_tiles = []
+        def regroup_piece(raw, part, vector_cols, label):
+            grouped = stage.tile([P, PIECE, PACK], BF16, align_bytes=64)
+            regroup(nc, grouped, raw[:, :, part * PIECE : (part + 1) * PIECE], vector_cols)
+            return grouped, mx_operand(keep, PIECE, label)
 
-        def load_next_weights():
-            if len(raw_tiles) < len(sources):
-                source = sources[len(raw_tiles)]
-                raw = raw_pool.tile([P, PACK, LOAD_COLS], BF16)
-                if source.ndim == 4:
-                    nc.sync.dma_start(out=raw[:].rearrange("p (u e) n -> p u e n", e=2), in_=source)
-                else:
-                    nc.sync.dma_start(out=raw[:], in_=source)
-                raw_tiles.append(raw)
-
-        for j in range(RAW_BUFS):
-            load_next_weights()
+        def quantise_piece(piece):
+            grouped, operand = piece
+            quantise(nc, operand, grouped[:].rearrange("p w t -> p (w t)"))
 
         w_cq_mx = []
+        waiting = None
         for c in range(PASSES_1):
-            raw = raw_tiles[c]
-            w_cq_mx.append(
-                [
-                    quantise_weight_piece(
-                        nc, stage, keep, raw[:, :, g * PIECE : (g + 1) * PIECE], VECTOR_COLS_W_CQ, "w_cq%d%d" % (c, g)
-                    )
-                    for g in range(PASSES_2)
-                ]
-            )
-            load_next_weights()
-
-        c_q_mx = []
-        for a in range(S_TILES):
-            c_q_grouped = small_stage.tile([P, PASSES_2, P, PACK], BF16, align_bytes=64)
+            w_cq_mx.append([])
             for g in range(PASSES_2):
-                c_q_bank = psum.tile([P, PACK, P], F32, tag="bank")
-                for t in range(PACK):
-                    for c in range(PASSES_1):
-                        multiply_mx(
-                            nc,
-                            c_q_bank[:, t, :],
-                            columns(w_cq_mx[c][g], t * P, P),
-                            columns(h_mx[a], c * P, P),
-                            first=(c == 0),
-                            last=(c == PASSES_1 - 1),
-                        )
-                nc.scalar.copy(out=c_q_grouped[:, g], in_=c_q_bank[:].rearrange("m t s -> m s t"))
-            codes = keep.tile([P, PASSES_2 * P], U32, align_bytes=64, name="c_q_codes%d" % a)
-            scales = keep.tile([P, PASSES_2 * P], U8, align_bytes=64, name="c_q_scales%d" % a)
-            quantise(nc, codes[:], scales[:], c_q_grouped[:].rearrange("m g s t -> m (g s t)"))
-            c_q_mx.append((codes, scales))
+                piece = regroup_piece(raw_tiles[c], g, VECTOR_COLS_BEFORE_ROPE, "w_cq%d%d" % (c, g))
+                w_cq_mx[c].append(piece[1])
+                if waiting is not None:
+                    quantise_piece(waiting)
+                waiting = piece
+            load_next_weights()
+        quantise_piece(waiting)
+        waiting = None
 
-        def quantise_group_weights(group):
-            half, part = divmod(group, LOAD_COLS // PIECE)
-            first_raw = PASSES_1 + half * 2 * PASSES_2
-            pieces = []
-            for j in range(2 * PASSES_2):
-                raw = raw_tiles[first_raw + j]
-                pieces.append(
-                    quantise_weight_piece(
+        sin_plus = const.tile([P, S_TILES, PAIRS], F32)
+        nc.vector.scalar_tensor_tensor(
+            out=sin_plus[:], in0=sin_half[:], scalar=2.0, in1=cos_half[:], op0=ALU.mult, op1=ALU.mult
+        )
+        sin_minus = const.tile([P, S_TILES, PAIRS], F32)
+        nc.vector.scalar_tensor_tensor(
+            out=sin_minus[:], in0=sin_half[:], scalar=-2.0, in1=cos_half[:], op0=ALU.mult, op1=ALU.mult
+        )
+
+        c_q_grouped = {}
+        c_q_mx = {}
+        w_mx = {}
+        products = {}
+        results = {}
+        out_rows = out.rearrange("b n (p a) d -> p (b n) a d", a=S_TILES)
+
+        def step_of(j):
+            half, rest = divmod(j, S_TILES * PARTS)
+            a, part = divmod(rest, PARTS)
+            return half, part, a
+
+        def c_q_bank(b):
+            a, g = divmod(b, PASSES_2)
+            bank = psum_c_q.tile([P, PACK, P], F32)
+            for t in range(PACK):
+                for c in range(PASSES_1):
+                    multiply_mx(
                         nc,
-                        stage,
-                        keep,
-                        raw[:, :, part * PIECE : (part + 1) * PIECE],
-                        VECTOR_COLS_BY_HALF[half],
-                        "w%d%d" % (group, j),
+                        bank[:, t, :],
+                        columns(w_cq_mx[c][g], t * P, P),
+                        columns(h_mx[a], c * P, P),
+                        first=(c == 0),
+                        last=(c == PASSES_1 - 1),
                     )
-                )
-            return pieces[:PASSES_2], pieces[PASSES_2:]
+            return bank
 
-        def multiply_by_weights(a, weights):
-            bank = psum.tile([P, GROUP_HEADS, D_HEAD], F32, tag="bank")
+        def copy_c_q_bank(b, bank):
+            a, g = divmod(b, PASSES_2)
+            if g == 0:
+                c_q_grouped[a] = c_q_stage.tile([P, PASSES_2, P, PACK], BF16, align_bytes=64, name="c_q_grouped")
+            nc.scalar.copy(out=c_q_grouped[a][:, g], in_=bank[:].rearrange("m t s -> m s t"))
+
+        def quantise_c_q(a):
+            c_q_mx[a] = mx_operand(keep, PASSES_2 * P, "c_q%d" % a)
+            quantise(nc, c_q_mx[a], c_q_grouped[a][:].rearrange("m g s t -> m (g s t)"))
+
+        def multiply_by_weights(j, weight, pool):
+            half, part, a = step_of(j)
+            bank = pool.tile([P, GROUP_HEADS, D_HEAD], F32, name="bank%d" % weight, tag="u_bank" if weight == 0 else "a_bank")
             for g in range(PASSES_2):
                 multiply_mx(
                     nc,
                     bank[:].rearrange("p n d -> p (n d)"),
                     columns(c_q_mx[a], g * P, P),
-                    columns(weights[g], 0, PIECE),
+                    columns(w_mx[(weight, half, part, g)], 0, PIECE),
                     first=(g == 0),
                     last=(g == PASSES_2 - 1),
                 )
             return bank
 
-        def rope_products(a, u_bank):
+        def rope_products(j, u_bank):
+            a = step_of(j)[2]
             pairs = [P, GROUP_HEADS, PAIRS]
             u_pairs = u_bank[:].rearrange("p n (i e) -> p n i e", e=2)
             by_cos = rope_pool.tile([P, GROUP_HEADS, D_HEAD], F32)
@@ -302,31 +310,54 @@ def tile_mla_pa_kernel(tc, h, w_cq, w_q, w_qr, out):
                 in1=sin_plus[:, a, :].unsqueeze(1).to_broadcast(pairs),
                 op=ALU.mult,
             )
-            return by_cos, by_sin
+            products[j] = (by_cos, by_sin)
 
-        out_rows = out.rearrange("b n (p a) d -> p (b n) a d", a=S_TILES)
-        group_weights = [quantise_group_weights(0)]
-        for group in range(GROUPS):
-            if group + 1 < GROUPS:
-                group_weights.append(quantise_group_weights(group + 1))
-            w_q_mx, w_qr_mx = group_weights[group]
-            for first_a in range(0, S_TILES, 2):
-                result = result_pool.tile([P, GROUP_HEADS, 2, 2 * D_HEAD], F32)
-                products = []
-                for x in range(2):
-                    a_bank = multiply_by_weights(first_a + x, w_q_mx)
-                    u_bank = multiply_by_weights(first_a + x, w_qr_mx)
-                    nc.scalar.copy(out=result[:, :, x, 0:D_HEAD], in_=a_bank[:])
-                    products.append(rope_products(first_a + x, u_bank))
-                for x in range(2):
-                    by_cos, by_sin = products[x]
-                    nc.vector.tensor_tensor(
-                        out=result[:, :, x, D_HEAD:].rearrange("p n (i e) -> p n i e", e=2),
-                        in0=by_cos[:].rearrange("p n (i e) -> p n i e", e=2),
-                        in1=by_sin[:].rearrange("p n e i -> p n i e"),
-                        op=ALU.add,
-                    )
-                nc.sync.dma_start(
-                    out=out_rows[:, group * GROUP_HEADS : (group + 1) * GROUP_HEADS, first_a : first_a + 2, :],
-                    in_=result[:],
+        def rope_sum(j):
+            by_cos, by_sin = products[j]
+            results[j] = result_pool.tile([P, GROUP_HEADS, 2 * D_HEAD], F32, name="result")
+            nc.vector.tensor_tensor(
+                out=results[j][:, :, D_HEAD:].rearrange("p n (i e) -> p n i e", e=2),
+                in0=by_cos[:].rearrange("p n (i e) -> p n i e", e=2),
+                in1=by_sin[:].rearrange("p n e i -> p n i e"),
+                op=ALU.add,
+            )
+
+        def store(j):
+            half, part, a = step_of(j)
+            first_head = (half * PARTS + part) * GROUP_HEADS
+            nc.sync.dma_start(out=out_rows[:, first_head : first_head + GROUP_HEADS, a, :], in_=results[j][:])
+
+        for i in range(STEPS + A_LAG):
+            u_step, a_step = i - U_LAG, i - A_LAG
+            if i < C_Q_BANKS:
+                new_c_q = c_q_bank(i)
+            if 0 <= u_step < STEPS:
+                u_bank = multiply_by_weights(u_step, 0, psum_u)
+            if 0 <= a_step:
+                a_bank = multiply_by_weights(a_step, 1, psum_a)
+            piece = None
+            if i < PIECES:
+                load, part = divmod(i, PARTS)
+                half, rest = divmod(load, 2 * PASSES_2)
+                weight, g = divmod(rest, PASSES_2)
+                piece = regroup_piece(
+                    raw_tiles[PASSES_1 + load],
+                    part,
+                    VECTOR_COLS_BEFORE_ROPE if i < U_LAG else VECTOR_COLS_BESIDE_ROPE,
+                    "w%d%d%d%d" % (weight, half, part, g),
                 )
+                w_mx[(weight, half, part, g)] = piece[1]
+            if waiting is not None:
+                quantise_piece(waiting)
+            waiting = piece
+            if i < C_Q_BANKS:
+                copy_c_q_bank(i, new_c_q)
+            if 0 < i <= C_Q_BANKS and i % PASSES_2 == 0:
+                quantise_c_q(i // PASSES_2 - 1)
+            if 0 <= u_step < STEPS:
+                rope_products(u_step, u_bank)
+            if 0 <= u_step - 1 < STEPS:
+                rope_sum(u_step - 1)
+            if 0 <= a_step:
+                nc.scalar.copy(out=results[a_step][:, :, 0:D_HEAD], in_=a_bank[:])
+                store(a_step)

@@ -42,14 +42,14 @@ A_LAG = 8
 
 RAW_BUFS = 8
 VECTOR_COLS_BEFORE_ROPE = 256
-VECTOR_COLS_BESIDE_ROPE = 48
+VECTOR_COLS_BESIDE_ROPE = 144
 
 ROUND_MAGIC = 1.5 * 2.0**23
 
 FLOPS = 2 * S * D_MODEL * D_CQ + 2 * S * D_CQ * 2 * HEADS * D_HEAD
 
 
-def rope_half_angles(nc, pool):
+def rope_half_angles(nc, pool, for_even, for_odd):
     shape = [P, S_TILES, PAIRS]
     position_int = pool.tile([P, S_TILES], I32)
     nc.gpsimd.iota(position_int[:], pattern=[[1, S_TILES]], base=0, channel_multiplier=S_TILES)
@@ -87,18 +87,12 @@ def rope_half_angles(nc, pool):
     nc.scalar.activation(out=sin_quarter[:], in_=turns[:], func=ACT.Sin, scale=math.pi / 2.0)
     square = pool.tile(shape, F32)
     nc.scalar.activation(out=square[:], in_=sin_half[:], func=ACT.Square)
-    cos_twice = pool.tile([P, S_TILES, D_HEAD], F32)
-    nc.scalar.activation(
-        out=cos_twice[:].rearrange("p a (i e) -> p (a i) e", e=2),
-        in_=square[:].rearrange("p a i -> p (a i)").unsqueeze(2).to_broadcast([P, S_TILES * PAIRS, 2]),
-        func=ACT.Copy,
-        scale=-2.0,
-        bias=1.0,
-    )
+    nc.scalar.activation(out=for_even[:, :, :, 0], in_=square[:], func=ACT.Copy, scale=-2.0, bias=1.0)
+    nc.scalar.activation(out=for_odd[:, :, :, 1], in_=square[:], func=ACT.Copy, scale=-2.0, bias=1.0)
     cos_half = pool.tile(shape, F32)
     nc.scalar.activation(out=cos_half[:], in_=sin_quarter[:], func=ACT.Square)
     nc.scalar.activation(out=cos_half[:], in_=cos_half[:], func=ACT.Copy, scale=-2.0, bias=1.0)
-    return sin_half, cos_half, cos_twice
+    return sin_half, cos_half
 
 
 def quantise(nc, operand, grouped):
@@ -153,7 +147,9 @@ def tile_mla_pa_kernel(tc, h, w_cq, w_q, w_qr, out):
 
         identity = const.tile([P, P], F32)
         make_identity(nc, identity[:])
-        sin_half, cos_half, cos_twice = rope_half_angles(nc, const)
+        for_even = const.tile([P, S_TILES, PAIRS, 2], F32)
+        for_odd = const.tile([P, S_TILES, PAIRS, 2], F32)
+        sin_half, cos_half = rope_half_angles(nc, const, for_even, for_odd)
 
         h_rows = h.flatten_outer_dims().rearrange("(p a) k -> p a k", a=S_TILES)
         h_mx = []
@@ -200,8 +196,15 @@ def tile_mla_pa_kernel(tc, h, w_cq, w_q, w_qr, out):
                     )
                 h_mx.append(mx_operand(keep, PASSES_1 * P, "h%d" % a))
                 quantise(nc, h_mx[a], h_grouped[:].rearrange("q c s t -> q (c s t)"))
-        rope_pool = ctx.enter_context(tc.tile_pool(name="rope_pool", bufs=3, reuse_waits="tile"))
+        rope_pool = ctx.enter_context(tc.tile_pool(name="rope_pool", bufs=4, reuse_waits="tile"))
         result_pool = ctx.enter_context(tc.tile_pool(name="result_pool", bufs=5, reuse_waits="tile"))
+
+        sin_x = const.tile([P, S_TILES, PAIRS], F32)
+        nc.vector.scalar_tensor_tensor(
+            out=sin_x[:], in0=sin_half[:], scalar=2.0, in1=cos_half[:], op0=ALU.mult, op1=ALU.mult
+        )
+        nc.scalar.copy(out=for_even[:, :, :, 1], in_=sin_x[:])
+        nc.scalar.mul(out=for_odd[:, :, :, 0], in_=sin_x[:], mul=-1.0)
 
         def regroup_piece(raw, part, vector_cols, label):
             grouped = stage.tile([P, PIECE, PACK], BF16, align_bytes=64)
@@ -225,15 +228,6 @@ def tile_mla_pa_kernel(tc, h, w_cq, w_q, w_qr, out):
             load_next_weights()
         quantise_piece(waiting)
         waiting = None
-
-        sin_plus = const.tile([P, S_TILES, PAIRS], F32)
-        nc.vector.scalar_tensor_tensor(
-            out=sin_plus[:], in0=sin_half[:], scalar=2.0, in1=cos_half[:], op0=ALU.mult, op1=ALU.mult
-        )
-        sin_minus = const.tile([P, S_TILES, PAIRS], F32)
-        nc.vector.scalar_tensor_tensor(
-            out=sin_minus[:], in0=sin_half[:], scalar=-2.0, in1=cos_half[:], op0=ALU.mult, op1=ALU.mult
-        )
 
         c_q_grouped = {}
         c_q_mx = {}
@@ -288,37 +282,31 @@ def tile_mla_pa_kernel(tc, h, w_cq, w_q, w_qr, out):
 
         def rope_products(j, u_bank):
             a = step_of(j)[2]
-            pairs = [P, GROUP_HEADS, PAIRS]
+            whole = [P, GROUP_HEADS, PAIRS, 2]
             u_pairs = u_bank[:].rearrange("p n (i e) -> p n i e", e=2)
-            by_cos = rope_pool.tile([P, GROUP_HEADS, D_HEAD], F32)
+            from_even = rope_pool.tile(whole, F32)
             nc.vector.tensor_tensor(
-                out=by_cos[:],
-                in0=u_bank[:],
-                in1=cos_twice[:, a, :].unsqueeze(1).to_broadcast([P, GROUP_HEADS, D_HEAD]),
+                out=from_even[:],
+                in0=u_pairs[:, :, :, 0:1].to_broadcast(whole),
+                in1=for_even[:, a].unsqueeze(1).to_broadcast(whole),
                 op=ALU.mult,
             )
-            by_sin = rope_pool.tile([P, GROUP_HEADS, 2, PAIRS], F32)
+            from_odd = rope_pool.tile(whole, F32)
             nc.vector.tensor_tensor(
-                out=by_sin[:, :, 0, :],
-                in0=u_pairs[:, :, :, 1],
-                in1=sin_minus[:, a, :].unsqueeze(1).to_broadcast(pairs),
+                out=from_odd[:],
+                in0=u_pairs[:, :, :, 1:2].to_broadcast(whole),
+                in1=for_odd[:, a].unsqueeze(1).to_broadcast(whole),
                 op=ALU.mult,
             )
-            nc.vector.tensor_tensor(
-                out=by_sin[:, :, 1, :],
-                in0=u_pairs[:, :, :, 0],
-                in1=sin_plus[:, a, :].unsqueeze(1).to_broadcast(pairs),
-                op=ALU.mult,
-            )
-            products[j] = (by_cos, by_sin)
+            products[j] = (from_even, from_odd)
 
         def rope_sum(j):
-            by_cos, by_sin = products[j]
+            from_even, from_odd = products[j]
             results[j] = result_pool.tile([P, GROUP_HEADS, 2 * D_HEAD], F32, name="result")
-            nc.vector.tensor_tensor(
-                out=results[j][:, :, D_HEAD:].rearrange("p n (i e) -> p n i e", e=2),
-                in0=by_cos[:].rearrange("p n (i e) -> p n i e", e=2),
-                in1=by_sin[:].rearrange("p n e i -> p n i e"),
+            nc.gpsimd.tensor_tensor(
+                out=results[j][:, :, D_HEAD:],
+                in0=from_even[:].rearrange("p n i e -> p n (i e)"),
+                in1=from_odd[:].rearrange("p n i e -> p n (i e)"),
                 op=ALU.add,
             )
 
@@ -356,8 +344,7 @@ def tile_mla_pa_kernel(tc, h, w_cq, w_q, w_qr, out):
                 quantise_c_q(i // PASSES_2 - 1)
             if 0 <= u_step < STEPS:
                 rope_products(u_step, u_bank)
-            if 0 <= u_step - 1 < STEPS:
-                rope_sum(u_step - 1)
+                rope_sum(u_step)
             if 0 <= a_step:
                 nc.scalar.copy(out=results[a_step][:, :, 0:D_HEAD], in_=a_bank[:])
                 store(a_step)

import math
from contextlib import ExitStack

import concourse.mybir as mybir
from concourse.masks import make_identity

F32 = mybir.dt.float32
BF16 = mybir.dt.bfloat16
I32 = mybir.dt.int32
U32 = mybir.dt.uint32
U8 = mybir.dt.uint8
FP8X4 = mybir.dt.float8_e4m3fn_x4
ALU = mybir.AluOpType
ACT = mybir.ActivationFunctionType

P = 128
PACK = 4
K_PASS = P * PACK

S = 512
D_MODEL = 2048
D_CQ = 1024
HEADS = 16
D_HEAD = 128
PAIRS = D_HEAD // 2
ROPE_BASE = 10000.0

S_TILES = S // P
PASSES_1 = D_MODEL // K_PASS
PASSES_2 = D_CQ // K_PASS
PIECE = 512
LOAD_COLS = 2 * PIECE
PARTS = LOAD_COLS // PIECE
GROUP_HEADS = PIECE // D_HEAD
HALVES = HEADS * D_HEAD // LOAD_COLS

C_Q_BANKS = S_TILES * PASSES_2
PIECES = 2 * PASSES_2 * HALVES * PARTS
STEPS = S_TILES * HALVES * PARTS
U_LAG = 4
A_LAG = 8

RAW_BUFS = 8
VECTOR_COLS_BEFORE_ROPE = 256
VECTOR_COLS_BESIDE_ROPE = 144

ROUND_MAGIC = 1.5 * 2.0**23

FLOPS = 2 * S * D_MODEL * D_CQ + 2 * S * D_CQ * 2 * HEADS * D_HEAD


def rope_half_angles(nc, pool, for_even, for_odd):
    shape = [P, S_TILES, PAIRS]
    position_int = pool.tile([P, S_TILES], I32)
    nc.gpsimd.iota(position_int[:], pattern=[[1, S_TILES]], base=0, channel_multiplier=S_TILES)
    position = pool.tile([P, S_TILES], F32)
    nc.vector.tensor_copy(out=position[:], in_=position_int[:])

    frequency = pool.tile([P, PAIRS], F32)
    nc.vector.memset(frequency[:, 0:1], 1.0)
    filled = 1
    while filled < PAIRS:
        nc.vector.tensor_scalar_mul(
            out=frequency[:, filled : 2 * filled],
            in0=frequency[:, 0:filled],
            scalar1=ROPE_BASE ** (-2.0 * filled / D_HEAD),
        )
        filled *= 2
    turns = pool.tile(shape, F32)
    nc.vector.scalar_tensor_tensor(
        out=turns[:],
        in0=frequency[:].unsqueeze(1).to_broadcast(shape),
        scalar=1.0 / (2.0 * math.pi),
        in1=position[:].unsqueeze(2).to_broadcast(shape),
        op0=ALU.mult,
        op1=ALU.mult,
    )
    whole_turns = pool.tile(shape, F32)
    nc.vector.tensor_scalar(
        out=whole_turns[:], in0=turns[:], scalar1=ROUND_MAGIC, scalar2=ROUND_MAGIC, op0=ALU.add, op1=ALU.subtract
    )
    nc.vector.tensor_tensor(out=turns[:], in0=turns[:], in1=whole_turns[:], op=ALU.subtract)

    sin_half = pool.tile(shape, F32)
    nc.scalar.activation(out=sin_half[:], in_=turns[:], func=ACT.Sin, scale=math.pi)
    sin_quarter = pool.tile(shape, F32)
    nc.scalar.activation(out=sin_quarter[:], in_=turns[:], func=ACT.Sin, scale=math.pi / 2.0)
    square = pool.tile(shape, F32)
    nc.scalar.activation(out=square[:], in_=sin_half[:], func=ACT.Square)
    nc.scalar.activation(out=for_even[:, :, :, 0], in_=square[:], func=ACT.Copy, scale=-2.0, bias=1.0)
    nc.scalar.activation(out=for_odd[:, :, :, 1], in_=square[:], func=ACT.Copy, scale=-2.0, bias=1.0)
    cos_half = pool.tile(shape, F32)
    nc.scalar.activation(out=cos_half[:], in_=sin_quarter[:], func=ACT.Square)
    nc.scalar.activation(out=cos_half[:], in_=cos_half[:], func=ACT.Copy, scale=-2.0, bias=1.0)
    return sin_half, cos_half


def quantise(nc, operand, grouped):
    nc.vector.quantize_mx(out=operand[0][:].bitcast(FP8X4), scales=operand[1][:], in_=grouped)


def mx_operand(pool, width, label):
    codes = pool.tile([P, width], U32, align_bytes=64, name=label + "_codes")
    scales = pool.tile([P, width], U8, align_bytes=64, name=label + "_scales")
    return codes, scales


def columns(operand, start, width):
    return operand[0][:, start : start + width], operand[1][:, start : start + width]


def multiply_mx(nc, acc, stationary, moving, first, last):
    nc.tensor.matmul_mx(
        out=acc,
        lhsT=stationary[0].bitcast(FP8X4),
        lhsT_scale=stationary[1],
        rhs=moving[0].bitcast(FP8X4),
        rhs_scale=moving[1],
        start=first,
        stop=last,
    )


def regroup(nc, grouped, raw_piece, vector_cols):
    nc.vector.tensor_copy(
        out=grouped[:, :vector_cols, :].rearrange("p (w i) t -> p w t i", i=4),
        in_=raw_piece[:, :, :vector_cols].rearrange("p t (w i) -> p w t i", i=4),
    )
    nc.scalar.copy(
        out=grouped[:, vector_cols:, :].rearrange("p (w i) t -> p w t i", i=4),
        in_=raw_piece[:, :, vector_cols:].rearrange("p t (w i) -> p w t i", i=4),
    )


def tile_mla_pa_kernel(tc, h, w_cq, w_q, w_qr, out):
    nc = tc.nc
    with ExitStack() as ctx:
        ctx.enter_context(tc.manual_schedule())
        const = ctx.enter_context(tc.tile_pool(name="const", bufs=1))
        keep = ctx.enter_context(tc.tile_pool(name="keep", bufs=1))
        raw_pool = ctx.enter_context(tc.tile_pool(name="raw_pool", bufs=RAW_BUFS))
        stage = ctx.enter_context(tc.tile_pool(name="stage", bufs=4))
        c_q_stage = ctx.enter_context(tc.tile_pool(name="c_q_stage", bufs=2))
        psum_u = ctx.enter_context(tc.psum_pool(name="psum_u", bufs=4))
        psum_a = ctx.enter_context(tc.psum_pool(name="psum_a", bufs=2))
        psum_c_q = ctx.enter_context(tc.psum_pool(name="psum_c_q", bufs=2))

        identity = const.tile([P, P], F32)
        make_identity(nc, identity[:])
        for_even = const.tile([P, S_TILES, PAIRS, 2], F32)
        for_odd = const.tile([P, S_TILES, PAIRS, 2], F32)
        sin_half, cos_half = rope_half_angles(nc, const, for_even, for_odd)

        h_rows = h.flatten_outer_dims().rearrange("(p a) k -> p a k", a=S_TILES)
        h_mx = []
        with tc.tile_pool(name="h_pool", bufs=S_TILES) as h_pool, tc.tile_pool(name="h_stage", bufs=2) as h_stage:
            h_raw = []
            for a in range(S_TILES):
                h_tile = h_pool.tile([P, D_MODEL], BF16)
                nc.sync.dma_start(out=h_tile[:], in_=h_rows[:, a, :])
                h_raw.append(h_tile)

            w_cq_rows = w_cq.rearrange("(c u p e) n -> c p u e n", c=PASSES_1, u=2, e=2)
            sources = [w_cq_rows[c] for c in range(PASSES_1)]
            for half in range(HALVES):
                for weight in (w_qr, w_q):
                    rows = weight.rearrange("(g t p) n -> g p t n", g=PASSES_2, t=PACK)
                    for g in range(PASSES_2):
                        sources.append(rows[g][:, :, half * LOAD_COLS : (half + 1) * LOAD_COLS])
            raw_tiles = []

            def load_next_weights():
                if len(raw_tiles) < len(sources):
                    source = sources[len(raw_tiles)]
                    raw = raw_pool.tile([P, PACK, LOAD_COLS], BF16)
                    if source.ndim == 4:
                        nc.sync.dma_start(out=raw[:].rearrange("p (u e) n -> p u e n", e=2), in_=source)
                    else:
                        nc.sync.dma_start(out=raw[:], in_=source)
                    raw_tiles.append(raw)

            for j in range(RAW_BUFS):
                load_next_weights()

            for a in range(S_TILES):
                h_words = h_raw[a][:].bitcast(F32)
                h_grouped = h_stage.tile([P, PASSES_1, P, PACK], BF16, align_bytes=64)
                for b in range(PASSES_1 // 2):
                    flipped = psum_u.tile([P, 4, P], F32, tag="u_bank")
                    for j in range(4):
                        first_word = (4 * b + j) * P
                        nc.tensor.transpose(flipped[:, j, :], h_words[:, first_word : first_word + P], identity[:])
                    nc.scalar.copy(
                        out=h_grouped[:, 2 * b : 2 * b + 2].bitcast(F32),
                        in_=flipped[:].rearrange("q (c u) s -> q c s u", u=2),
                    )
                h_mx.append(mx_operand(keep, PASSES_1 * P, "h%d" % a))
                quantise(nc, h_mx[a], h_grouped[:].rearrange("q c s t -> q (c s t)"))
        rope_pool = ctx.enter_context(tc.tile_pool(name="rope_pool", bufs=4, reuse_waits="tile"))
        result_pool = ctx.enter_context(tc.tile_pool(name="result_pool", bufs=5, reuse_waits="tile"))

        sin_x = const.tile([P, S_TILES, PAIRS], F32)
        nc.vector.scalar_tensor_tensor(
            out=sin_x[:], in0=sin_half[:], scalar=2.0, in1=cos_half[:], op0=ALU.mult, op1=ALU.mult
        )
        nc.scalar.copy(out=for_even[:, :, :, 1], in_=sin_x[:])
        nc.scalar.mul(out=for_odd[:, :, :, 0], in_=sin_x[:], mul=-1.0)

        def regroup_piece(raw, part, vector_cols, label):
            grouped = stage.tile([P, PIECE, PACK], BF16, align_bytes=64)
            regroup(nc, grouped, raw[:, :, part * PIECE : (part + 1) * PIECE], vector_cols)
            return grouped, mx_operand(keep, PIECE, label)

        def quantise_piece(piece):
            grouped, operand = piece
            quantise(nc, operand, grouped[:].rearrange("p w t -> p (w t)"))

        w_cq_mx = []
        waiting = None
        for c in range(PASSES_1):
            w_cq_mx.append([])
            for g in range(PASSES_2):
                piece = regroup_piece(raw_tiles[c], g, VECTOR_COLS_BEFORE_ROPE, "w_cq%d%d" % (c, g))
                w_cq_mx[c].append(piece[1])
                if waiting is not None:
                    quantise_piece(waiting)
                waiting = piece
            load_next_weights()
        quantise_piece(waiting)
        waiting = None

        c_q_grouped = {}
        c_q_mx = {}
        w_mx = {}
        products = {}
        results = {}
        out_rows = out.rearrange("b n (p a) d -> p (b n) a d", a=S_TILES)

        def step_of(j):
            half, rest = divmod(j, S_TILES * PARTS)
            a, part = divmod(rest, PARTS)
            return half, part, a

        def c_q_bank(b):
            a, g = divmod(b, PASSES_2)
            bank = psum_c_q.tile([P, PACK, P], F32)
            for t in range(PACK):
                for c in range(PASSES_1):
                    multiply_mx(
                        nc,
                        bank[:, t, :],
                        columns(w_cq_mx[c][g], t * P, P),
                        columns(h_mx[a], c * P, P),
                        first=(c == 0),
                        last=(c == PASSES_1 - 1),
                    )
            return bank

        def copy_c_q_bank(b, bank):
            a, g = divmod(b, PASSES_2)
            if g == 0:
                c_q_grouped[a] = c_q_stage.tile([P, PASSES_2, P, PACK], BF16, align_bytes=64, name="c_q_grouped")
            nc.scalar.copy(out=c_q_grouped[a][:, g], in_=bank[:].rearrange("m t s -> m s t"))

        def quantise_c_q(a):
            c_q_mx[a] = mx_operand(keep, PASSES_2 * P, "c_q%d" % a)
            quantise(nc, c_q_mx[a], c_q_grouped[a][:].rearrange("m g s t -> m (g s t)"))

        def multiply_by_weights(j, weight, pool):
            half, part, a = step_of(j)
            bank = pool.tile([P, GROUP_HEADS, D_HEAD], F32, name="bank%d" % weight, tag="u_bank" if weight == 0 else "a_bank")
            for g in range(PASSES_2):
                multiply_mx(
                    nc,
                    bank[:].rearrange("p n d -> p (n d)"),
                    columns(c_q_mx[a], g * P, P),
                    columns(w_mx[(weight, half, part, g)], 0, PIECE),
                    first=(g == 0),
                    last=(g == PASSES_2 - 1),
                )
            return bank

        def rope_products(j, u_bank):
            a = step_of(j)[2]
            whole = [P, GROUP_HEADS, PAIRS, 2]
            u_pairs = u_bank[:].rearrange("p n (i e) -> p n i e", e=2)
            from_even = rope_pool.tile(whole, F32)
            nc.vector.tensor_tensor(
                out=from_even[:],
                in0=u_pairs[:, :, :, 0:1].to_broadcast(whole),
                in1=for_even[:, a].unsqueeze(1).to_broadcast(whole),
                op=ALU.mult,
            )
            from_odd = rope_pool.tile(whole, F32)
            nc.vector.tensor_tensor(
                out=from_odd[:],
                in0=u_pairs[:, :, :, 1:2].to_broadcast(whole),
                in1=for_odd[:, a].unsqueeze(1).to_broadcast(whole),
                op=ALU.mult,
            )
            products[j] = (from_even, from_odd)

        def rope_sum(j):
            from_even, from_odd = products[j]
            results[j] = result_pool.tile([P, GROUP_HEADS, 2 * D_HEAD], F32, name="result")
            nc.gpsimd.tensor_tensor(
                out=results[j][:, :, D_HEAD:],
                in0=from_even[:].rearrange("p n i e -> p n (i e)"),
                in1=from_odd[:].rearrange("p n i e -> p n (i e)"),
                op=ALU.add,
            )

        def store(j):
            half, part, a = step_of(j)
            first_head = (half * PARTS + part) * GROUP_HEADS
            nc.sync.dma_start(out=out_rows[:, first_head : first_head + GROUP_HEADS, a, :], in_=results[j][:])

        for i in range(STEPS + A_LAG):
            u_step, a_step = i - U_LAG, i - A_LAG
            if i < C_Q_BANKS:
                new_c_q = c_q_bank(i)
            if 0 <= u_step < STEPS:
                u_bank = multiply_by_weights(u_step, 0, psum_u)
            if 0 <= a_step:
                a_bank = multiply_by_weights(a_step, 1, psum_a)
            piece = None
            if i < PIECES:
                load, part = divmod(i, PARTS)
                half, rest = divmod(load, 2 * PASSES_2)
                weight, g = divmod(rest, PASSES_2)
                piece = regroup_piece(
                    raw_tiles[PASSES_1 + load],
                    part,
                    VECTOR_COLS_BEFORE_ROPE if i < U_LAG else VECTOR_COLS_BESIDE_ROPE,
                    "w%d%d%d%d" % (weight, half, part, g),
                )
                w_mx[(weight, half, part, g)] = piece[1]
            if waiting is not None:
                quantise_piece(waiting)
            waiting = piece
            if i < C_Q_BANKS:
                copy_c_q_bank(i, new_c_q)
            if 0 < i <= C_Q_BANKS and i % PASSES_2 == 0:
                quantise_c_q(i // PASSES_2 - 1)
            if 0 <= u_step < STEPS:
                rope_products(u_step, u_bank)
                rope_sum(u_step)
            if 0 <= a_step:
                nc.scalar.copy(out=results[a_step][:, :, 0:D_HEAD], in_=a_bank[:])
                store(a_step)
